import numpy as np
import ml_dtypes


def mxq(x, axis, fmt="e4m3"):
    dtype, down = {"e4m3": (ml_dtypes.float8_e4m3fn, 7), "e5m2": (ml_dtypes.float8_e5m2, 14)}[fmt]
    v = np.moveaxis(np.asarray(x, np.float32).astype(ml_dtypes.bfloat16).astype(np.float64), axis, -1)
    blocks = v.reshape(v.shape[:-1] + (-1, 32))
    amax = np.abs(blocks).max(-1, keepdims=True)
    byte = np.maximum(np.where(amax > 0, np.frexp(amax)[1] - 1 + 127, 0) - down, 1)
    scale = np.exp2(byte - 127.0)
    codes = (blocks / scale).astype(np.float32).astype(dtype).astype(np.float64)
    return np.moveaxis((codes * scale).reshape(v.shape), -1, axis)


WIDE = False


def mx_kscale(k):
    if not WIDE:
        return np.ones(k)
    levels = np.array([10, -10, 5, -5, 0])
    if k % 512:
        return np.exp2(np.random.permutation(np.resize(levels, k // 32))).repeat(32)
    a = np.empty((k // 512, 16))
    for p in range(k // 512):
        a[p, :8] = np.random.permutation(np.resize(levels, 8))
        for g in range(8):
            far = levels[np.abs(levels - a[p, g]) >= 10]
            a[p, g + 8] = far[np.random.randint(len(far))]
    return np.exp2(a.ravel()).repeat(32)


BF16 = ml_dtypes.bfloat16


def bf(x):
    return np.asarray(x, np.float32).astype(BF16)


def f64(x):
    return np.asarray(x).astype(np.float64)


N, G, F, K, E = 512, 4096, 128, 4, 1


def setup_inputs():
    s = mx_kscale(N)
    return {"x": bf(np.random.standard_normal((N, G)) * s[:, None]),
            "S": bf(np.random.standard_normal((E, N, N)) / np.sqrt(N) / s[:, None] * s[None, :])}


def reference(x, S):
    Sq = mxq(f64(S), 1, "e4m3")
    z0 = np.broadcast_to(f64(x).T[None], (E, G, N))
    z1 = mxq(z0, 2, "e4m3") @ Sq
    z2 = mxq(z1, 2, "e4m3") @ Sq
    return z1, z2

@@ -1,0 +1,221 @@
+from contextlib import ExitStack
+
+import concourse.mybir as mybir
+
+F32 = mybir.dt.float32
+BF16 = mybir.dt.bfloat16
+U32 = mybir.dt.uint32
+U8 = mybir.dt.uint8
+FP8X4 = mybir.dt.float8_e4m3fn_x4
+
+P = 128
+PACK = 4
+NODES = 512
+FEATS = 4096
+CHUNK = 512
+ROWS = 4
+NCHUNK = FEATS // CHUNK
+LOAD_WIDTHS = (512, 512, 1024, 2048)
+FLOPS = 2 * 2 * FEATS * NODES * NODES
+
+
+def tile_graphfilter_pa_t_kernel(tc, x, S, out_0, out_1):
+    nc = tc.nc
+    x_view = x.rearrange("(p t) g -> p t g", t=PACK)
+    s_view = S[0, :, :].rearrange("(p t) n -> p t n", t=PACK)
+    z1_view = out_0[0, :, :].rearrange("(c m r) j -> c m r j", m=P, r=ROWS)
+    z2_view = out_1[0, :, :].rearrange("(c m r) j -> c m r j", m=P, r=ROWS)
+
+    with ExitStack() as ctx:
+        keep = ctx.enter_context(tc.tile_pool(name="keep", bufs=1))
+        grp = ctx.enter_context(tc.tile_pool(name="grp", bufs=3))
+        stage = ctx.enter_context(tc.tile_pool(name="stage", bufs=8))
+        psum_t = ctx.enter_context(tc.psum_pool(name="psum_t", bufs=4))
+        psum_o = ctx.enter_context(tc.psum_pool(name="psum_o", bufs=4))
+        ctx.enter_context(tc.manual_schedule())
+
+        s_raw = keep.tile([P, PACK, NODES], BF16, name="s_raw")
+        x_raw = []
+        start = 0
+        for i, width in enumerate(LOAD_WIDTHS):
+            raw = keep.tile([P, PACK, width], BF16, name="x_raw%d" % i)
+            nc.sync.dma_start(out=raw[:], in_=x_view[:, :, start : start + width])
+            if i == 0:
+                nc.sync.dma_start(out=s_raw[:], in_=s_view)
+            for k in range(width // CHUNK):
+                x_raw.append(raw[:, :, k * CHUNK : (k + 1) * CHUNK])
+            start += width
+
+        s_grp = keep.tile([P, NODES, PACK], BF16, name="s_grp", align_bytes=64)
+        s_codes = keep.tile([P, NODES], U32, name="s_codes", align_bytes=64)
+        s_scales = keep.tile([P, NODES], U8, name="s_scales", align_bytes=64)
+
+        x_grp = {}
+        x_codes = {}
+        x_scales = {}
+        z_grp = {}
+        z_codes = {}
+        z_scales = {}
+        zt_bank = {}
+        out_bank = {}
+        out_stage = {}
+
+        def regroup_x(c, engine, lo, hi):
+            if c not in x_grp:
+                tag = "x_grp" if c >= 1 else "x_grp0"
+                x_grp[c] = keep.tile([P, ROWS, P, PACK], BF16, name="x_grp_%d" % c, tag=tag, align_bytes=64)
+            dst = x_grp[c][:, :, lo:hi, :].rearrange("p r m t -> p m t r")
+            src = x_raw[c][:, :, ROWS * lo : ROWS * hi].rearrange("p t (m r) -> p m t r", r=ROWS)
+            if engine == "vector":
+                nc.vector.tensor_copy(out=dst, in_=src)
+            elif engine == "scalar":
+                nc.scalar.copy(out=dst, in_=src)
+            else:
+                nc.gpsimd.tensor_scalar(
+                    out=dst, in0=src, scalar1=1.0, scalar2=0.0,
+                    op0=mybir.AluOpType.mult, op1=mybir.AluOpType.add,
+                )
+
+        def quantise_x(c):
+            x_codes[c] = keep.tile([P, CHUNK], U32, name="x_codes%d" % c, align_bytes=64)
+            x_scales[c] = keep.tile([P, CHUNK], U8, name="x_scales%d" % c, align_bytes=64)
+            nc.vector.quantize_mx(
+                out=x_codes[c][:].bitcast(FP8X4),
+                scales=x_scales[c][:],
+                in_=x_grp[c][:].rearrange("p r m t -> p (r m t)"),
+            )
+
+        def shift_transposed(c, r):
+            cols = slice(r * P, (r + 1) * P)
+            bank = psum_t.tile([P, PACK, P], F32, name="zt%d_%d" % (c, r), tag="zt")
+            zt_bank[(c, r)] = bank
+            for t in range(PACK):
+                nodes = slice(t * P, (t + 1) * P)
+                nc.tensor.matmul_mx(
+                    out=bank[:, t, :],
+                    lhsT=s_codes[:, nodes].bitcast(FP8X4),
+                    lhsT_scale=s_scales[:, nodes],
+                    rhs=x_codes[c][:, cols].bitcast(FP8X4),
+                    rhs_scale=x_scales[c][:, cols],
+                    start=True,
+                    stop=True,
+                )
+
+        def shift(which, codes, scales, c, r):
+            cols = slice(r * P, (r + 1) * P)
+            bank = psum_o.tile([P, NODES], F32, name="zo%d_%d_%d" % (which, c, r), tag="zo")
+            out_bank[(which, c, r)] = bank
+            nc.tensor.matmul_mx(
+                out=bank[:],
+                lhsT=codes[c][:, cols].bitcast(FP8X4),
+                lhsT_scale=scales[c][:, cols],
+                rhs=s_codes[:].bitcast(FP8X4),
+                rhs_scale=s_scales[:],
+                start=True,
+                stop=True,
+            )
+
+        def regroup_z(c, r):
+            if r == 0:
+                z_grp[c] = grp.tile([P, ROWS, P, PACK], BF16, name="z_grp%d" % c, tag="z_grp", align_bytes=64)
+            nc.vector.tensor_copy(
+                out=z_grp[c][:, r, :, :],
+                in_=zt_bank[(c, r)][:].rearrange("p t g -> p g t"),
+            )
+
+        def quantise_z(c):
+            z_codes[c] = keep.tile([P, CHUNK], U32, name="z_codes%d" % c, align_bytes=64)
+            z_scales[c] = keep.tile([P, CHUNK], U8, name="z_scales%d" % c, align_bytes=64)
+            nc.vector.quantize_mx(
+                out=z_codes[c][:].bitcast(FP8X4),
+                scales=z_scales[c][:],
+                in_=z_grp[c][:].rearrange("p r m t -> p (r m t)"),
+            )
+
+        def empty(which, c, r, engine):
+            if (which, c) not in out_stage:
+                out_stage[(which, c)] = stage.tile([P, ROWS, NODES], F32, name="st%d_%d" % (which, c), tag="st")
+            dst = out_stage[(which, c)][:, r, :].rearrange("p (m t) -> p m t", t=PACK)
+            src = out_bank[(which, c, r)][:].rearrange("p (t m) -> p m t", t=PACK)
+            if engine == "scalar":
+                nc.scalar.copy(out=dst, in_=src)
+            else:
+                nc.vector.tensor_copy(out=dst, in_=src)
+
+        def store(which, c, lo, hi):
+            view = z1_view if which == 1 else z2_view
+            nc.sync.dma_start(out=view[c][:, lo:hi, :], in_=out_stage[(which, c)][:, lo:hi, :])
+
+        HALF = P // 2
+        s_dst = s_grp[:].rearrange("p (t m) j -> p m j t", t=PACK)
+        s_src = s_raw[:].rearrange("p j (m t) -> p m j t", t=PACK)
+        SPLIT = 80
+        regroup_x(0, "vector", 0, P)
+        nc.vector.tensor_copy(out=s_dst[:, :HALF, :, :], in_=s_src[:, :HALF, :, :])
+        nc.scalar.copy(out=s_dst[:, HALF:, :, :], in_=s_src[:, HALF:, :, :])
+        quantise_x(0)
+        nc.vector.quantize_mx(
+            out=s_codes[:].bitcast(FP8X4),
+            scales=s_scales[:],
+            in_=s_grp[:].rearrange("p n t -> p (n t)"),
+        )
+        regroup_x(1, "scalar", 0, 64)
+        regroup_x(1, "vector", 64, P)
+        for r in range(ROWS):
+            shift_transposed(0, r)
+            shift(1, x_codes, x_scales, 0, r)
+
+        regroup_z(0, 0)
+        quantise_x(1)
+        regroup_x(2, "gpsimd", 0, 48)
+        for r in range(ROWS):
+            empty(1, 0, r, "scalar")
+        store(1, 0, 0, ROWS)
+        for r in range(ROWS):
+            if r > 0:
+                regroup_z(0, r)
+            shift_transposed(1, r)
+            shift(1, x_codes, x_scales, 1, r)
+        for r in range(ROWS):
+            empty(1, 1, r, "scalar")
+        store(1, 1, 0, ROWS)
+        quantise_z(0)
+        regroup_x(2, "vector", 48, P)
+        quantise_x(2)
+
+        for c in range(1, NCHUNK):
+            if c + 2 < NCHUNK:
+                regroup_x(c + 2, "gpsimd", 0, SPLIT)
+            for r in range(ROWS):
+                shift(2, z_codes, z_scales, c - 1, r)
+            for r in range(ROWS):
+                empty(2, c - 1, r, "scalar")
+            store(2, c - 1, 0, ROWS)
+            for r in range(ROWS):
+                regroup_z(c, r)
+                if c + 1 < NCHUNK:
+                    shift_transposed(c + 1, r)
+                    shift(1, x_codes, x_scales, c + 1, r)
+            if c + 1 < NCHUNK:
+                helped = c % 2 == 0
+                if helped:
+                    empty(1, c + 1, 0, "vector")
+                for r in range(ROWS):
+                    if not (helped and r == 0):
+                        empty(1, c + 1, r, "scalar")
+                store(1, c + 1, 0, ROWS)
+            if c + 2 < NCHUNK:
+                regroup_x(c + 2, "vector", SPLIT, P)
+            quantise_z(c)
+            if c + 2 < NCHUNK:
+                quantise_x(c + 2)
+
+        last = NCHUNK - 1
+        for r in range(ROWS):
+            shift(2, z_codes, z_scales, last, r)
+        empty(2, last, 0, "scalar")
+        empty(2, last, 1, "vector")
+        store(2, last, 0, 2)
+        empty(2, last, 2, "scalar")
+        empty(2, last, 3, "vector")
+        store(2, last, 2, 4)

@@ -15,7 +15,8 @@ FEATS = 4096
 CHUNK = 512
 ROWS = 4
 NCHUNK = FEATS // CHUNK
-LOAD_WIDTHS = (512, 512, 1024, 2048)
+GROUPS = ((0,), (1,), (2,), (3,), (4,), (5,), (6,), (7,))
+LOADS = ((0,), (1,), (2, 3), (4, 5, 6, 7))
 FLOPS = 2 * 2 * FEATS * NODES * NODES
 
 
@@ -23,28 +24,31 @@ def tile_graphfilter_pa_t_kernel(tc, x, S, out_0, out_1):
     nc = tc.nc
     x_view = x.rearrange("(p t) g -> p t g", t=PACK)
     s_view = S[0, :, :].rearrange("(p t) n -> p t n", t=PACK)
-    z1_view = out_0[0, :, :].rearrange("(c m r) j -> c m r j", m=P, r=ROWS)
-    z2_view = out_1[0, :, :].rearrange("(c m r) j -> c m r j", m=P, r=ROWS)
+    outs = {1: out_0, 2: out_1}
+    group_of = {c: g for g in GROUPS for c in g}
 
     with ExitStack() as ctx:
         keep = ctx.enter_context(tc.tile_pool(name="keep", bufs=1))
         grp = ctx.enter_context(tc.tile_pool(name="grp", bufs=3))
-        stage = ctx.enter_context(tc.tile_pool(name="stage", bufs=8))
+        stage = ctx.enter_context(tc.tile_pool(name="stage", bufs=6))
+        stage2 = ctx.enter_context(tc.tile_pool(name="stage2", bufs=4))
         psum_t = ctx.enter_context(tc.psum_pool(name="psum_t", bufs=4))
         psum_o = ctx.enter_context(tc.psum_pool(name="psum_o", bufs=4))
         ctx.enter_context(tc.manual_schedule())
 
         s_raw = keep.tile([P, PACK, NODES], BF16, name="s_raw")
-        x_raw = []
-        start = 0
-        for i, width in enumerate(LOAD_WIDTHS):
+        x_raw = {}
+        for i, chunks in enumerate(LOADS):
+            lo = CHUNK * chunks[0]
+            width = CHUNK * len(chunks)
             raw = keep.tile([P, PACK, width], BF16, name="x_raw%d" % i)
-            nc.sync.dma_start(out=raw[:], in_=x_view[:, :, start : start + width])
+            nc.sync.dma_start(out=raw[:], in_=x_view[:, :, lo : lo + width])
             if i == 0:
                 nc.sync.dma_start(out=s_raw[:], in_=s_view)
-            for k in range(width // CHUNK):
-                x_raw.append(raw[:, :, k * CHUNK : (k + 1) * CHUNK])
-            start += width
+            for c in chunks:
+                g = group_of[c]
+                at = CHUNK * (g[0] - chunks[0])
+                x_raw[c] = raw[:, :, at : at + CHUNK * len(g)]
 
         s_grp = keep.tile([P, NODES, PACK], BF16, name="s_grp", align_bytes=64)
         s_codes = keep.tile([P, NODES], U32, name="s_codes", align_bytes=64)
@@ -60,12 +64,22 @@ def tile_graphfilter_pa_t_kernel(tc, x, S, out_0, out_1):
         out_bank = {}
         out_stage = {}
 
+        def regroup_s(engine, lo, hi):
+            dst = s_grp[:].rearrange("p (t m) j -> p m j t", t=PACK)[:, lo:hi, :, :]
+            src = s_raw[:].rearrange("p j (m t) -> p m j t", t=PACK)[:, lo:hi, :, :]
+            if engine == "vector":
+                nc.vector.tensor_copy(out=dst, in_=src)
+            else:
+                nc.scalar.copy(out=dst, in_=src)
+
         def regroup_x(c, engine, lo, hi):
+            rows = ROWS * len(group_of[c])
+            first = ROWS * group_of[c].index(c)
             if c not in x_grp:
                 tag = "x_grp" if c >= 1 else "x_grp0"
                 x_grp[c] = keep.tile([P, ROWS, P, PACK], BF16, name="x_grp_%d" % c, tag=tag, align_bytes=64)
             dst = x_grp[c][:, :, lo:hi, :].rearrange("p r m t -> p m t r")
-            src = x_raw[c][:, :, ROWS * lo : ROWS * hi].rearrange("p t (m r) -> p m t r", r=ROWS)
+            src = x_raw[c].rearrange("p t (m r) -> p m t r", r=rows)[:, lo:hi, :, first : first + ROWS]
             if engine == "vector":
                 nc.vector.tensor_copy(out=dst, in_=src)
             elif engine == "scalar":
@@ -75,6 +89,13 @@ def tile_graphfilter_pa_t_kernel(tc, x, S, out_0, out_1):
                     out=dst, in0=src, scalar1=1.0, scalar2=0.0,
                     op0=mybir.AluOpType.mult, op1=mybir.AluOpType.add,
                 )
+
+        def quantise_s():
+            nc.vector.quantize_mx(
+                out=s_codes[:].bitcast(FP8X4),
+                scales=s_scales[:],
+                in_=s_grp[:].rearrange("p n j -> p (n j)"),
+            )
 
         def quantise_x(c):
             x_codes[c] = keep.tile([P, CHUNK], U32, name="x_codes%d" % c, align_bytes=64)
@@ -101,7 +122,9 @@ def tile_graphfilter_pa_t_kernel(tc, x, S, out_0, out_1):
                     stop=True,
                 )
 
-        def shift(which, codes, scales, c, r):
+        def shift(which, c, r):
+            codes = x_codes if which == 1 else z_codes
+            scales = x_scales if which == 1 else z_scales
             cols = slice(r * P, (r + 1) * P)
             bank = psum_o.tile([P, NODES], F32, name="zo%d_%d_%d" % (which, c, r), tag="zo")
             out_bank[(which, c, r)] = bank
@@ -133,9 +156,12 @@ def tile_graphfilter_pa_t_kernel(tc, x, S, out_0, out_1):
             )
 
         def empty(which, c, r, engine):
-            if (which, c) not in out_stage:
-                out_stage[(which, c)] = stage.tile([P, ROWS, NODES], F32, name="st%d_%d" % (which, c), tag="st")
-            dst = out_stage[(which, c)][:, r, :].rearrange("p (m t) -> p m t", t=PACK)
+            g = group_of[c]
+            row = ROWS * g.index(c) + r
+            if (which, g) not in out_stage:
+                pool = stage if len(g) == 1 else stage2
+                out_stage[(which, g)] = pool.tile([P, ROWS * len(g), NODES], F32, name="st%d_%d" % (which, c), tag="st%d" % len(g))
+            dst = out_stage[(which, g)][:, row, :].rearrange("p (m t) -> p m t", t=PACK)
             src = out_bank[(which, c, r)][:].rearrange("p (t m) -> p m t", t=PACK)
             if engine == "scalar":
                 nc.scalar.copy(out=dst, in_=src)
@@ -143,42 +169,63 @@ def tile_graphfilter_pa_t_kernel(tc, x, S, out_0, out_1):
                 nc.vector.tensor_copy(out=dst, in_=src)
 
         def store(which, c, lo, hi):
-            view = z1_view if which == 1 else z2_view
-            nc.sync.dma_start(out=view[c][:, lo:hi, :], in_=out_stage[(which, c)][:, lo:hi, :])
+            g = group_of[c]
+            feats = slice(CHUNK * g[0], CHUNK * (g[0] + len(g)))
+            view = outs[which][0, feats, :].rearrange("(m r) j -> m r j", r=ROWS * len(g))
+            nc.sync.dma_start(out=view[:, lo:hi, :], in_=out_stage[(which, g)][:, lo:hi, :])
 
-        HALF = P // 2
-        s_dst = s_grp[:].rearrange("p (t m) j -> p m j t", t=PACK)
-        s_src = s_raw[:].rearrange("p j (m t) -> p m j t", t=PACK)
+        def store_group(which, c):
+            g = group_of[c]
+            if which == 2 and g == GROUPS[-1]:
+                first = ROWS * g.index(c)
+                store(which, c, first, first + ROWS)
+            elif c == g[-1]:
+                store(which, c, 0, ROWS * len(g))
+
+        def warm_up(count):
+            bank = psum_t.tile([P, NODES], F32, name="warm", tag="zt")
+            for i in range(count):
+                nc.tensor.matmul(
+                    out=bank[:],
+                    lhsT=x_raw[0][:, i % PACK, :P],
+                    rhs=x_raw[0][:, i % PACK, :],
+                    start=True,
+                    stop=True,
+                )
+
         SPLIT = 80
-        regroup_x(0, "vector", 0, P)
-        nc.vector.tensor_copy(out=s_dst[:, :HALF, :, :], in_=s_src[:, :HALF, :, :])
-        nc.scalar.copy(out=s_dst[:, HALF:, :, :], in_=s_src[:, HALF:, :, :])
+        warm_up(6)
+        regroup_x(0, "scalar", 0, 32)
+        regroup_x(0, "vector", 32, P)
         quantise_x(0)
-        nc.vector.quantize_mx(
-            out=s_codes[:].bitcast(FP8X4),
-            scales=s_scales[:],
-            in_=s_grp[:].rearrange("p n t -> p (n t)"),
-        )
-        regroup_x(1, "scalar", 0, 64)
-        regroup_x(1, "vector", 64, P)
-        for r in range(ROWS):
-            shift_transposed(0, r)
-            shift(1, x_codes, x_scales, 0, r)
+        regroup_s("scalar", 0, 64)
+        regroup_s("vector", 64, P)
+        quantise_s()
+        regroup_x(1, "scalar", 0, 48)
+        regroup_x(1, "vector", 48, P)
+        shift(1, 0, 0)
+        shift(1, 0, 1)
+        shift_transposed(0, 0)
+        shift(1, 0, 2)
+        shift_transposed(0, 1)
+        shift(1, 0, 3)
+        shift_transposed(0, 2)
+        shift_transposed(0, 3)
 
         regroup_z(0, 0)
         quantise_x(1)
         regroup_x(2, "gpsimd", 0, 48)
         for r in range(ROWS):
             empty(1, 0, r, "scalar")
-        store(1, 0, 0, ROWS)
+        store_group(1, 0)
         for r in range(ROWS):
             if r > 0:
                 regroup_z(0, r)
+            shift(1, 1, r)
             shift_transposed(1, r)
-            shift(1, x_codes, x_scales, 1, r)
         for r in range(ROWS):
             empty(1, 1, r, "scalar")
-        store(1, 1, 0, ROWS)
+        store_group(1, 1)
         quantise_z(0)
         regroup_x(2, "vector", 48, P)
         quantise_x(2)
@@ -187,15 +234,15 @@ def tile_graphfilter_pa_t_kernel(tc, x, S, out_0, out_1):
             if c + 2 < NCHUNK:
                 regroup_x(c + 2, "gpsimd", 0, SPLIT)
             for r in range(ROWS):
-                shift(2, z_codes, z_scales, c - 1, r)
+                shift(2, c - 1, r)
             for r in range(ROWS):
                 empty(2, c - 1, r, "scalar")
-            store(2, c - 1, 0, ROWS)
+            store_group(2, c - 1)
             for r in range(ROWS):
                 regroup_z(c, r)
                 if c + 1 < NCHUNK:
                     shift_transposed(c + 1, r)
-                    shift(1, x_codes, x_scales, c + 1, r)
+                    shift(1, c + 1, r)
             if c + 1 < NCHUNK:
                 helped = c % 2 == 0
                 if helped:
@@ -203,7 +250,7 @@ def tile_graphfilter_pa_t_kernel(tc, x, S, out_0, out_1):
                 for r in range(ROWS):
                     if not (helped and r == 0):
                         empty(1, c + 1, r, "scalar")
-                store(1, c + 1, 0, ROWS)
+                store_group(1, c + 1)
             if c + 2 < NCHUNK:
                 regroup_x(c + 2, "vector", SPLIT, P)
             quantise_z(c)
@@ -212,10 +259,11 @@ def tile_graphfilter_pa_t_kernel(tc, x, S, out_0, out_1):
 
         last = NCHUNK - 1
         for r in range(ROWS):
-            shift(2, z_codes, z_scales, last, r)
+            shift(2, last, r)
         empty(2, last, 0, "scalar")
         empty(2, last, 1, "vector")
-        store(2, last, 0, 2)
+        first = ROWS * group_of[last].index(last)
+        store(2, last, first, first + 2)
         empty(2, last, 2, "scalar")
         empty(2, last, 3, "vector")
-        store(2, last, 2, 4)
+        store(2, last, first + 2, first + 4)

@@ -36,12 +36,12 @@ def tile_graphfilter_pa_t_kernel(tc, x, S, out_0, out_1):
         psum_o = ctx.enter_context(tc.psum_pool(name="psum_o", bufs=4))
         ctx.enter_context(tc.manual_schedule())
 
-        s_raw = keep.tile([P, PACK, NODES], BF16, name="s_raw")
+        s_raw = keep.tile([P, PACK, NODES], BF16, name="s_raw", align_bytes=256)
         x_raw = {}
         for i, chunks in enumerate(LOADS):
             lo = CHUNK * chunks[0]
             width = CHUNK * len(chunks)
-            raw = keep.tile([P, PACK, width], BF16, name="x_raw%d" % i)
+            raw = keep.tile([P, PACK, width], BF16, name="x_raw%d" % i, align_bytes=256)
             nc.sync.dma_start(out=raw[:], in_=x_view[:, :, lo : lo + width])
             if i == 0:
                 nc.sync.dma_start(out=s_raw[:], in_=s_view)
@@ -160,7 +160,9 @@ def tile_graphfilter_pa_t_kernel(tc, x, S, out_0, out_1):
             row = ROWS * g.index(c) + r
             if (which, g) not in out_stage:
                 pool = stage if len(g) == 1 else stage2
-                out_stage[(which, g)] = pool.tile([P, ROWS * len(g), NODES], F32, name="st%d_%d" % (which, c), tag="st%d" % len(g))
+                out_stage[(which, g)] = pool.tile(
+                    [P, ROWS * len(g), NODES], F32, name="st%d_%d" % (which, c), tag="st%d" % len(g), align_bytes=256
+                )
             dst = out_stage[(which, g)][:, row, :].rearrange("p (m t) -> p m t", t=PACK)
             src = out_bank[(which, c, r)][:].rearrange("p (t m) -> p m t", t=PACK)
             if engine == "scalar":

@@ -199,9 +199,9 @@ def tile_graphfilter_pa_t_kernel(tc, x, S, out_0, out_1):
         warm_up(6)
         regroup_x(0, "scalar", 0, 32)
         regroup_x(0, "vector", 32, P)
-        quantise_x(0)
         regroup_s("scalar", 0, 64)
         regroup_s("vector", 64, P)
+        quantise_x(0)
         quantise_s()
         regroup_x(1, "scalar", 0, 48)
         regroup_x(1, "vector", 48, P)
@@ -214,9 +214,9 @@ def tile_graphfilter_pa_t_kernel(tc, x, S, out_0, out_1):
         shift_transposed(0, 2)
         shift_transposed(0, 3)
 
-        regroup_z(0, 0)
         quantise_x(1)
-        regroup_x(2, "gpsimd", 0, 48)
+        regroup_z(0, 0)
+        regroup_x(2, "gpsimd", 0, 64)
         for r in range(ROWS):
             empty(1, 0, r, "scalar")
         store_group(1, 0)
@@ -229,7 +229,7 @@ def tile_graphfilter_pa_t_kernel(tc, x, S, out_0, out_1):
             empty(1, 1, r, "scalar")
         store_group(1, 1)
         quantise_z(0)
-        regroup_x(2, "vector", 48, P)
+        regroup_x(2, "vector", 64, P)
         quantise_x(2)
 
         for c in range(1, NCHUNK):

@@ -173,8 +173,10 @@ def tile_graphfilter_pa_t_kernel(tc, x, S, out_0, out_1):
         def store(which, c, lo, hi):
             g = group_of[c]
             feats = slice(CHUNK * g[0], CHUNK * (g[0] + len(g)))
-            view = outs[which][0, feats, :].rearrange("(m r) j -> m r j", r=ROWS * len(g))
-            nc.sync.dma_start(out=view[:, lo:hi, :], in_=out_stage[(which, g)][:, lo:hi, :])
+            view = outs[which][0, feats, :].rearrange("(m r) j -> m (r j)", r=ROWS * len(g))
+            rows = out_stage[(which, g)][:].rearrange("p r j -> p (r j)")
+            span = slice(lo * NODES, hi * NODES)
+            nc.sync.dma_start(out=view[:, span], in_=rows[:, span])
 
         def store_group(which, c):
             g = group_of[c]
@@ -195,16 +197,16 @@ def tile_graphfilter_pa_t_kernel(tc, x, S, out_0, out_1):
                     stop=True,
                 )
 
-        SPLIT = 80
+        SPLIT = 96
         warm_up(6)
         regroup_x(0, "scalar", 0, 32)
         regroup_x(0, "vector", 32, P)
-        regroup_s("scalar", 0, 64)
-        regroup_s("vector", 64, P)
+        regroup_s("scalar", 0, 56)
+        regroup_s("vector", 56, P)
         quantise_x(0)
         quantise_s()
-        regroup_x(1, "scalar", 0, 48)
-        regroup_x(1, "vector", 48, P)
+        regroup_x(1, "scalar", 0, 32)
+        regroup_x(1, "vector", 32, P)
         shift(1, 0, 0)
         shift(1, 0, 1)
         shift_transposed(0, 0)
@@ -212,24 +214,25 @@ def tile_graphfilter_pa_t_kernel(tc, x, S, out_0, out_1):
         shift_transposed(0, 1)
         shift(1, 0, 3)
         shift_transposed(0, 2)
-        shift_transposed(0, 3)
 
         quantise_x(1)
         regroup_z(0, 0)
-        regroup_x(2, "gpsimd", 0, 64)
+        regroup_x(2, "gpsimd", 0, 80)
         for r in range(ROWS):
             empty(1, 0, r, "scalar")
         store_group(1, 0)
-        for r in range(ROWS):
-            if r > 0:
-                regroup_z(0, r)
+        shift(1, 1, 0)
+        shift_transposed(0, 3)
+        for r in range(1, ROWS):
+            regroup_z(0, r)
             shift(1, 1, r)
+        for r in range(ROWS):
             shift_transposed(1, r)
         for r in range(ROWS):
             empty(1, 1, r, "scalar")
         store_group(1, 1)
         quantise_z(0)
-        regroup_x(2, "vector", 64, P)
+        regroup_x(2, "vector", 80, P)
         quantise_x(2)
 
         for c in range(1, NCHUNK):
@@ -265,7 +268,6 @@ def tile_graphfilter_pa_t_kernel(tc, x, S, out_0, out_1):
         empty(2, last, 0, "scalar")
         empty(2, last, 1, "vector")
         first = ROWS * group_of[last].index(last)
-        store(2, last, first, first + 2)
         empty(2, last, 2, "scalar")
         empty(2, last, 3, "vector")
-        store(2, last, first + 2, first + 4)
+        store(2, last, first, first + 4)

@@ -178,6 +178,18 @@ def tile_graphfilter_pa_t_kernel(tc, x, S, out_0, out_1):
             span = slice(lo * NODES, hi * NODES)
             nc.sync.dma_start(out=view[:, span], in_=rows[:, span])
 
+        HALVED = {1: (2,), 2: (0, 1)}
+
+        def empty_all(which, c):
+            for r in range(ROWS):
+                empty(which, c, r, "scalar")
+                if r == 1 and c in HALVED[which]:
+                    store(which, c, 0, 2)
+            if c in HALVED[which]:
+                store(which, c, 2, 4)
+            else:
+                store_group(which, c)
+
         def store_group(which, c):
             g = group_of[c]
             if which == 2 and g == GROUPS[-1]:
@@ -197,7 +209,7 @@ def tile_graphfilter_pa_t_kernel(tc, x, S, out_0, out_1):
                     stop=True,
                 )
 
-        SPLIT = 96
+        SPLIT = 112
         warm_up(6)
         regroup_x(0, "scalar", 0, 32)
         regroup_x(0, "vector", 32, P)
@@ -218,9 +230,7 @@ def tile_graphfilter_pa_t_kernel(tc, x, S, out_0, out_1):
         quantise_x(1)
         regroup_z(0, 0)
         regroup_x(2, "gpsimd", 0, 80)
-        for r in range(ROWS):
-            empty(1, 0, r, "scalar")
-        store_group(1, 0)
+        empty_all(1, 0)
         shift(1, 1, 0)
         shift_transposed(0, 3)
         for r in range(1, ROWS):
@@ -228,9 +238,7 @@ def tile_graphfilter_pa_t_kernel(tc, x, S, out_0, out_1):
             shift(1, 1, r)
         for r in range(ROWS):
             shift_transposed(1, r)
-        for r in range(ROWS):
-            empty(1, 1, r, "scalar")
-        store_group(1, 1)
+        empty_all(1, 1)
         quantise_z(0)
         regroup_x(2, "vector", 80, P)
         quantise_x(2)
@@ -240,22 +248,22 @@ def tile_graphfilter_pa_t_kernel(tc, x, S, out_0, out_1):
                 regroup_x(c + 2, "gpsimd", 0, SPLIT)
             for r in range(ROWS):
                 shift(2, c - 1, r)
-            for r in range(ROWS):
-                empty(2, c - 1, r, "scalar")
-            store_group(2, c - 1)
+            empty_all(2, c - 1)
             for r in range(ROWS):
                 regroup_z(c, r)
                 if c + 1 < NCHUNK:
                     shift_transposed(c + 1, r)
                     shift(1, c + 1, r)
             if c + 1 < NCHUNK:
-                helped = c % 2 == 0
+                helped = c > 1
                 if helped:
                     empty(1, c + 1, 0, "vector")
-                for r in range(ROWS):
-                    if not (helped and r == 0):
+                if helped:
+                    for r in range(1, ROWS):
                         empty(1, c + 1, r, "scalar")
-                store_group(1, c + 1)
+                    store_group(1, c + 1)
+                else:
+                    empty_all(1, c + 1)
             if c + 2 < NCHUNK:
                 regroup_x(c + 2, "vector", SPLIT, P)
             quantise_z(c)

from contextlib import ExitStack

import concourse.mybir as mybir

F32 = mybir.dt.float32
BF16 = mybir.dt.bfloat16
U32 = mybir.dt.uint32
U8 = mybir.dt.uint8
FP8X4 = mybir.dt.float8_e4m3fn_x4

P = 128
PACK = 4
NODES = 512
FEATS = 4096
CHUNK = 512
ROWS = 4
NCHUNK = FEATS // CHUNK
GROUPS = ((0,), (1,), (2,), (3,), (4,), (5,), (6,), (7,))
LOADS = ((0,), (1,), (2, 3), (4, 5, 6, 7))
FLOPS = 2 * 2 * FEATS * NODES * NODES


def tile_graphfilter_pa_t_kernel(tc, x, S, out_0, out_1):
    nc = tc.nc
    x_view = x.rearrange("(p t) g -> p t g", t=PACK)
    s_view = S[0, :, :].rearrange("(p t) n -> p t n", t=PACK)
    outs = {1: out_0, 2: out_1}
    group_of = {c: g for g in GROUPS for c in g}

    with ExitStack() as ctx:
        keep = ctx.enter_context(tc.tile_pool(name="keep", bufs=1))
        grp = ctx.enter_context(tc.tile_pool(name="grp", bufs=3))
        stage = ctx.enter_context(tc.tile_pool(name="stage", bufs=6))
        stage2 = ctx.enter_context(tc.tile_pool(name="stage2", bufs=4))
        psum_t = ctx.enter_context(tc.psum_pool(name="psum_t", bufs=4))
        psum_o = ctx.enter_context(tc.psum_pool(name="psum_o", bufs=4))
        ctx.enter_context(tc.manual_schedule())

        s_raw = keep.tile([P, PACK, NODES], BF16, name="s_raw", align_bytes=256)
        x_raw = {}
        for i, chunks in enumerate(LOADS):
            lo = CHUNK * chunks[0]
            width = CHUNK * len(chunks)
            raw = keep.tile([P, PACK, width], BF16, name="x_raw%d" % i, align_bytes=256)
            nc.sync.dma_start(out=raw[:], in_=x_view[:, :, lo : lo + width])
            if i == 0:
                nc.sync.dma_start(out=s_raw[:], in_=s_view)
            for c in chunks:
                g = group_of[c]
                at = CHUNK * (g[0] - chunks[0])
                x_raw[c] = raw[:, :, at : at + CHUNK * len(g)]

        s_grp = keep.tile([P, NODES, PACK], BF16, name="s_grp", align_bytes=64)
        s_codes = keep.tile([P, NODES], U32, name="s_codes", align_bytes=64)
        s_scales = keep.tile([P, NODES], U8, name="s_scales", align_bytes=64)

        x_grp = {}
        x_codes = {}
        x_scales = {}
        z_grp = {}
        z_codes = {}
        z_scales = {}
        zt_bank = {}
        out_bank = {}
        out_stage = {}

        def regroup_s(engine, lo, hi):
            dst = s_grp[:].rearrange("p (t m) j -> p m j t", t=PACK)[:, lo:hi, :, :]
            src = s_raw[:].rearrange("p j (m t) -> p m j t", t=PACK)[:, lo:hi, :, :]
            if engine == "vector":
                nc.vector.tensor_copy(out=dst, in_=src)
            else:
                nc.scalar.copy(out=dst, in_=src)

        def regroup_x(c, engine, lo, hi):
            rows = ROWS * len(group_of[c])
            first = ROWS * group_of[c].index(c)
            if c not in x_grp:
                tag = "x_grp" if c >= 1 else "x_grp0"
                x_grp[c] = keep.tile([P, ROWS, P, PACK], BF16, name="x_grp_%d" % c, tag=tag, align_bytes=64)
            dst = x_grp[c][:, :, lo:hi, :].rearrange("p r m t -> p m t r")
            src = x_raw[c].rearrange("p t (m r) -> p m t r", r=rows)[:, lo:hi, :, first : first + ROWS]
            if engine == "vector":
                nc.vector.tensor_copy(out=dst, in_=src)
            elif engine == "scalar":
                nc.scalar.copy(out=dst, in_=src)
            else:
                nc.gpsimd.tensor_scalar(
                    out=dst, in0=src, scalar1=1.0, scalar2=0.0,
                    op0=mybir.AluOpType.mult, op1=mybir.AluOpType.add,
                )

        def quantise_s():
            nc.vector.quantize_mx(
                out=s_codes[:].bitcast(FP8X4),
                scales=s_scales[:],
                in_=s_grp[:].rearrange("p n j -> p (n j)"),
            )

        def quantise_x(c):
            x_codes[c] = keep.tile([P, CHUNK], U32, name="x_codes%d" % c, align_bytes=64)
            x_scales[c] = keep.tile([P, CHUNK], U8, name="x_scales%d" % c, align_bytes=64)
            nc.vector.quantize_mx(
                out=x_codes[c][:].bitcast(FP8X4),
                scales=x_scales[c][:],
                in_=x_grp[c][:].rearrange("p r m t -> p (r m t)"),
            )

        def shift_transposed(c, r):
            cols = slice(r * P, (r + 1) * P)
            bank = psum_t.tile([P, PACK, P], F32, name="zt%d_%d" % (c, r), tag="zt")
            zt_bank[(c, r)] = bank
            for t in range(PACK):
                nodes = slice(t * P, (t + 1) * P)
                nc.tensor.matmul_mx(
                    out=bank[:, t, :],
                    lhsT=s_codes[:, nodes].bitcast(FP8X4),
                    lhsT_scale=s_scales[:, nodes],
                    rhs=x_codes[c][:, cols].bitcast(FP8X4),
                    rhs_scale=x_scales[c][:, cols],
                    start=True,
                    stop=True,
                )

        def shift(which, c, r):
            codes = x_codes if which == 1 else z_codes
            scales = x_scales if which == 1 else z_scales
            cols = slice(r * P, (r + 1) * P)
            bank = psum_o.tile([P, NODES], F32, name="zo%d_%d_%d" % (which, c, r), tag="zo")
            out_bank[(which, c, r)] = bank
            nc.tensor.matmul_mx(
                out=bank[:],
                lhsT=codes[c][:, cols].bitcast(FP8X4),
                lhsT_scale=scales[c][:, cols],
                rhs=s_codes[:].bitcast(FP8X4),
                rhs_scale=s_scales[:],
                start=True,
                stop=True,
            )

        def regroup_z(c, r):
            if r == 0:
                z_grp[c] = grp.tile([P, ROWS, P, PACK], BF16, name="z_grp%d" % c, tag="z_grp", align_bytes=64)
            nc.vector.tensor_copy(
                out=z_grp[c][:, r, :, :],
                in_=zt_bank[(c, r)][:].rearrange("p t g -> p g t"),
            )

        def quantise_z(c):
            z_codes[c] = keep.tile([P, CHUNK], U32, name="z_codes%d" % c, align_bytes=64)
            z_scales[c] = keep.tile([P, CHUNK], U8, name="z_scales%d" % c, align_bytes=64)
            nc.vector.quantize_mx(
                out=z_codes[c][:].bitcast(FP8X4),
                scales=z_scales[c][:],
                in_=z_grp[c][:].rearrange("p r m t -> p (r m t)"),
            )

        def empty(which, c, r, engine):
            g = group_of[c]
            row = ROWS * g.index(c) + r
            if (which, g) not in out_stage:
                pool = stage if len(g) == 1 else stage2
                out_stage[(which, g)] = pool.tile(
                    [P, ROWS * len(g), NODES], F32, name="st%d_%d" % (which, c), tag="st%d" % len(g), align_bytes=256
                )
            dst = out_stage[(which, g)][:, row, :].rearrange("p (m t) -> p m t", t=PACK)
            src = out_bank[(which, c, r)][:].rearrange("p (t m) -> p m t", t=PACK)
            if engine == "scalar":
                nc.scalar.copy(out=dst, in_=src)
            else:
                nc.vector.tensor_copy(out=dst, in_=src)

        def store(which, c, lo, hi):
            g = group_of[c]
            feats = slice(CHUNK * g[0], CHUNK * (g[0] + len(g)))
            view = outs[which][0, feats, :].rearrange("(m r) j -> m (r j)", r=ROWS * len(g))
            rows = out_stage[(which, g)][:].rearrange("p r j -> p (r j)")
            span = slice(lo * NODES, hi * NODES)
            nc.sync.dma_start(out=view[:, span], in_=rows[:, span])

        HALVED = {1: (2,), 2: (0, 1)}

        def empty_all(which, c):
            for r in range(ROWS):
                empty(which, c, r, "scalar")
                if r == 1 and c in HALVED[which]:
                    store(which, c, 0, 2)
            if c in HALVED[which]:
                store(which, c, 2, 4)
            else:
                store_group(which, c)

        def store_group(which, c):
            g = group_of[c]
            if which == 2 and g == GROUPS[-1]:
                first = ROWS * g.index(c)
                store(which, c, first, first + ROWS)
            elif c == g[-1]:
                store(which, c, 0, ROWS * len(g))

        def warm_up(count):
            bank = psum_t.tile([P, NODES], F32, name="warm", tag="zt")
            for i in range(count):
                nc.tensor.matmul(
                    out=bank[:],
                    lhsT=x_raw[0][:, i % PACK, :P],
                    rhs=x_raw[0][:, i % PACK, :],
                    start=True,
                    stop=True,
                )

        SPLIT = 112
        warm_up(6)
        regroup_x(0, "scalar", 0, 32)
        regroup_x(0, "vector", 32, P)
        regroup_s("scalar", 0, 56)
        regroup_s("vector", 56, P)
        quantise_x(0)
        quantise_s()
        regroup_x(1, "scalar", 0, 32)
        regroup_x(1, "vector", 32, P)
        shift(1, 0, 0)
        shift(1, 0, 1)
        shift_transposed(0, 0)
        shift(1, 0, 2)
        shift_transposed(0, 1)
        shift(1, 0, 3)
        shift_transposed(0, 2)

        quantise_x(1)
        regroup_z(0, 0)
        regroup_x(2, "gpsimd", 0, 80)
        empty_all(1, 0)
        shift(1, 1, 0)
        shift_transposed(0, 3)
        for r in range(1, ROWS):
            regroup_z(0, r)
            shift(1, 1, r)
        for r in range(ROWS):
            shift_transposed(1, r)
        empty_all(1, 1)
        quantise_z(0)
        regroup_x(2, "vector", 80, P)
        quantise_x(2)

        for c in range(1, NCHUNK):
            if c + 2 < NCHUNK:
                regroup_x(c + 2, "gpsimd", 0, SPLIT)
            for r in range(ROWS):
                shift(2, c - 1, r)
            empty_all(2, c - 1)
            for r in range(ROWS):
                regroup_z(c, r)
                if c + 1 < NCHUNK:
                    shift_transposed(c + 1, r)
                    shift(1, c + 1, r)
            if c + 1 < NCHUNK:
                helped = c > 1
                if helped:
                    empty(1, c + 1, 0, "vector")
                if helped:
                    for r in range(1, ROWS):
                        empty(1, c + 1, r, "scalar")
                    store_group(1, c + 1)
                else:
                    empty_all(1, c + 1)
            if c + 2 < NCHUNK:
                regroup_x(c + 2, "vector", SPLIT, P)
            quantise_z(c)
            if c + 2 < NCHUNK:
                quantise_x(c + 2)

        last = NCHUNK - 1
        for r in range(ROWS):
            shift(2, last, r)
        empty(2, last, 0, "scalar")
        empty(2, last, 1, "vector")
        first = ROWS * group_of[last].index(last)
        empty(2, last, 2, "scalar")
        empty(2, last, 3, "vector")
        store(2, last, first, first + 4)
